import numpy as np
import ml_dtypes


def mxq(x, axis, fmt="e4m3"):
    dtype, down = {"e4m3": (ml_dtypes.float8_e4m3fn, 7), "e5m2": (ml_dtypes.float8_e5m2, 14)}[fmt]
    v = np.moveaxis(np.asarray(x, np.float32).astype(ml_dtypes.bfloat16).astype(np.float64), axis, -1)
    blocks = v.reshape(v.shape[:-1] + (-1, 32))
    amax = np.abs(blocks).max(-1, keepdims=True)
    byte = np.maximum(np.where(amax > 0, np.frexp(amax)[1] - 1 + 127, 0) - down, 1)
    scale = np.exp2(byte - 127.0)
    codes = (blocks / scale).astype(np.float32).astype(dtype).astype(np.float64)
    return np.moveaxis((codes * scale).reshape(v.shape), -1, axis)


WIDE = False


def mx_kscale(k):
    if not WIDE:
        return np.ones(k)
    levels = np.array([10, -10, 5, -5, 0])
    a = np.random.permutation(np.resize(levels, k // 512 * 4)).reshape(k // 512, 4)
    idx = np.arange(k)
    return np.exp2(a[idx // 512, idx % 128 // 32])


BF16 = ml_dtypes.bfloat16


def bf(x):
    return np.asarray(x, np.float32).astype(BF16)


def f64(x):
    return np.asarray(x).astype(np.float64)


E2M1 = np.array([0.0, 0.5, 1.0, 1.5, 2.0, 3.0, 4.0, 6.0, -0.0, -0.5, -1.0, -1.5, -2.0, -3.0, -4.0, -6.0])


def pack_weight(w, fmt):
    k, n = w.shape
    w = f64(bf(w)).reshape(k // 32, 32, n)
    amax = np.abs(w).max(1)
    if fmt == "e4m3":
        byte = np.frexp(amax)[1] - 1 + 127 - 7
    else:
        mant, ex = np.frexp(amax / 6.0)
        byte = np.where(mant > 0.5, ex, ex - 1) + 127
    byte = np.clip(np.where(amax > 0, byte, 1), 1, 254)
    scaled = (w * np.exp2(127.0 - byte)[:, None, :]).reshape(k, n).astype(np.float32)
    by_word = np.ascontiguousarray(scaled.reshape(k // 512, 128, 4, n).transpose(0, 1, 3, 2))
    if fmt == "e4m3":
        words = by_word.astype(ml_dtypes.float8_e4m3fn).view(np.uint8)
    else:
        c = by_word.astype(ml_dtypes.float4_e2m1fn).view(np.uint8) & 0xF
        words = c[..., 0::2] | (c[..., 1::2] << 4)
    return np.ascontiguousarray(words), np.ascontiguousarray(byte.astype(np.uint8).reshape(k // 512, 16, n))


def unpack_weight(words, scales, fmt):
    g, p, n, _ = words.shape
    if fmt == "e4m3":
        vals = np.ascontiguousarray(words).view(ml_dtypes.float8_e4m3fn).astype(np.float64)
    else:
        nib = np.empty((g, p, n, 4), np.uint8)
        nib[..., 0::2] = words & 0xF
        nib[..., 1::2] = words >> 4
        vals = E2M1[nib]
    vals = vals * np.repeat(np.exp2(scales.astype(np.float64) - 127.0), 8, axis=1)[..., None]
    return vals.transpose(0, 1, 3, 2).reshape(g * 512, n)


B, C, H, W, KS, CO = 2, 512, 10, 10, 3, 4096
OH, OW = H - KS + 1, W - KS + 1
Q = C * KS * KS


def unfold_patches(x, k):
    oh, ow = x.shape[2] - k + 1, x.shape[3] - k + 1
    rows = []
    for di in range(k):
        cols = [x[:, :, di:di + oh, dj:dj + ow] for dj in range(k)]
        rows.append(np.stack(cols, axis=-1))
    return np.stack(rows, axis=-2)


def wide_factors():
    s = mx_kscale(Q)
    hi, lo = np.log2(s.max()), np.log2(s.min())
    n = np.arange(C)
    phi = np.exp2(np.round(hi + (lo - hi) * np.minimum(n, C - n) / (C / 2)))
    c, h, w = np.ogrid[:C, :H, :W]
    m, di, dj = np.ogrid[:C, :KS, :KS]
    return phi[(c * OH * OW + h * OW + w) % C], phi[(m + di * OW + dj) % C].reshape(Q)


def setup_inputs():
    fx, fw = wide_factors()
    x = bf(np.random.standard_normal((B, C, H, W)) * fx)
    words, scales = pack_weight(np.random.standard_normal((Q, CO)) / np.sqrt(Q) / fw[:, None], "e4m3")
    bias = bf(np.random.standard_normal(CO) * 0.3)
    return {"x": x, "weights_words": words, "weights_scales": scales, "bias": bias}


def reference(x, weights_words, weights_scales, bias):
    patches = unfold_patches(f64(x), KS)
    patches = patches.reshape(B, OH, OW, Q)
    out = (mxq(patches, 3, "e4m3") @ unpack_weight(weights_words, weights_scales, "e4m3")) + f64(bias)
    return np.transpose(out, (0, 3, 1, 2))

@@ -1,0 +1,194 @@
+from contextlib import ExitStack
+
+import concourse.mybir as mybir
+from concourse.masks import make_identity
+
+F32 = mybir.dt.float32
+BF16 = mybir.dt.bfloat16
+I32 = mybir.dt.int32
+U32 = mybir.dt.uint32
+U8 = mybir.dt.uint8
+FP8X4 = mybir.dt.float8_e4m3fn_x4
+
+P = 128
+G = 9
+CO = 4096
+NB = 8
+NT = 512
+FLOPS = 2 * 128 * 4608 * 4096
+
+TAIL_CHUNKS = [[0, 1], [2, 3], [4, 5], [6], [7]]
+G_HEAD = 7
+
+
+def tile_conv2d_w_kernel(tc, x, weights_words, weights_scales, bias, out):
+    nc = tc.nc
+    with ExitStack() as ctx:
+        keep = ctx.enter_context(tc.tile_pool(name="keep", bufs=1))
+        ypool = ctx.enter_context(tc.tile_pool(name="ypool", bufs=8))
+        opool = ctx.enter_context(tc.tile_pool(name="opool", bufs=8))
+        psum = ctx.enter_context(tc.psum_pool(name="psum", bufs=1))
+        ctx.enter_context(tc.manual_schedule())
+
+        xf = x.rearrange("b (r c) h w -> (b r) (c h w)", c=8)
+        ww = weights_words.rearrange("g p n t -> g p (n t)").bitcast(I32)
+        sc = weights_scales.bitcast(I32)
+        ov = out.rearrange("b (c m t) u v -> c m b (t u v)", c=NB, m=P, t=4)
+
+        xs = keep.tile([P, 3, 800], BF16, name="xs")
+        a_rows = keep.tile([P, 4608], BF16, name="a_rows", align_bytes=64)
+        grouped = keep.tile([P, G, P, 4], BF16, name="grouped", align_bytes=64)
+        a_codes = keep.tile([P, G, P], U32, name="a_codes", align_bytes=64)
+        a_scales = keep.tile([P, G, P], U8, name="a_scales", align_bytes=64)
+        ident = keep.tile([P, P], F32, name="ident")
+        bias_raw = keep.tile([P, NT], BF16, name="bias_raw")
+        bias_f = keep.tile([P, 4, P], F32, name="bias_f")
+        bias_t = keep.tile([P, NB, 4], F32, name="bias_t")
+        plane_a = keep.tile([P, CO], U8, name="plane_a", align_bytes=64)
+        plane_b = keep.tile([P, CO], U8, name="plane_b", align_bytes=64)
+        plane_c = keep.tile([P, CO // 4], U8, name="plane_c", align_bytes=64)
+        w_head = [
+            keep.tile([P, CO], I32, name="w_head%d" % g, align_bytes=64) for g in range(G_HEAD)
+        ]
+        w_tail = keep.tile([P, G - G_HEAD, CO], I32, name="w_tail", align_bytes=64)
+
+        nc.vector.memset(plane_a[:].bitcast(I32), 0)
+        nc.vector.memset(plane_b[:].bitcast(I32), 0)
+        nc.vector.memset(plane_c[:].bitcast(I32), 0)
+        make_identity(nc, ident[:])
+        nc.gpsimd.memset(bias_f[:], 0.0)
+
+        for dj in range(3):
+            nc.sync.dma_start(out=xs[:, dj, 0:798], in_=xf[:, dj : dj + 798])
+        nc.scalar.dma_start(out=bias_raw[0:NB, :], in_=bias.rearrange("(c n) -> c n", c=NB))
+        for plane, g0 in ((plane_a, 0), (plane_b, 4)):
+            for q in (0, 2, 1, 3):
+                nc.sync.dma_start(
+                    out=plane[32 * q : 32 * q + 16, :].bitcast(I32),
+                    in_=sc[g0 : g0 + 4, 4 * q : 4 * q + 4, :],
+                )
+        for q in (0, 2, 1, 3):
+            nc.sync.dma_start(
+                out=plane_c[32 * q : 32 * q + 16, :].bitcast(I32),
+                in_=sc[8, 4 * q : 4 * q + 4, :].rearrange("r (c n) -> c r n", c=4),
+            )
+        for g in range(G_HEAD):
+            nc.sync.dma_start(out=w_head[g][:], in_=ww[g])
+        for chunk in TAIL_CHUNKS:
+            cols = slice(NT * chunk[0], NT * (chunk[-1] + 1))
+            nc.sync.dma_start(
+                out=w_tail[:, :, cols], in_=ww[G_HEAD:G, :, cols].rearrange("g p n -> p g n")
+            )
+
+        xv = xs[:].rearrange("p b (c h w) -> p b c h w", c=8, h=10, w=10)
+        av = a_rows[:].rearrange("p (c i j a b) -> p c i j a b", c=8, i=8, j=8, a=3, b=3)
+        a_words = a_rows[:].bitcast(F32)
+        g_words = grouped[:].rearrange("p g c t -> p (g c t)").bitcast(F32).rearrange(
+            "p (g c u) -> p g c u", g=G, c=P, u=2
+        )
+
+        def patches(half):
+            for i in range(8):
+                nc.vector.tensor_copy(
+                    out=av[:, 4 * half : 4 * half + 4, i],
+                    in_=xv[:, :, 4 * half : 4 * half + 4, i : i + 3, 0:8].rearrange(
+                        "p b c a j -> p c j a b"
+                    ),
+                )
+
+        def flip(pair):
+            gs = [g for g in (2 * pair, 2 * pair + 1) if g < G]
+            xt = psum.tile([P, 2, 2, P], F32, name="xt%d" % pair, tag="bank%d" % pair)
+            for s, g in enumerate(gs):
+                for u in range(2):
+                    nc.tensor.transpose(
+                        xt[:, s, u, :], a_words[:, 256 * g + u : 256 * (g + 1) : 2], ident[:]
+                    )
+            nc.scalar.copy(
+                out=g_words[:, gs[0] : gs[-1] + 1],
+                in_=xt[:, 0 : len(gs)].rearrange("p g u c -> p g c u"),
+            )
+
+        def quantise(g0, g1):
+            nc.vector.quantize_mx(
+                out=a_codes[:, g0:g1, :].rearrange("p g c -> p (g c)").bitcast(FP8X4),
+                scales=a_scales[:, g0:g1, :].rearrange("p g c -> p (g c)"),
+                in_=grouped[:, g0:g1].rearrange("p g c t -> p (g c t)"),
+            )
+
+        patches(0)
+        flip(0)
+        flip(1)
+        nc.vector.tensor_copy(
+            out=bias_f[0:NB], in_=bias_raw[0:NB, :].rearrange("c (m t) -> c t m", t=4)
+        )
+        bt = psum.tile([P, 4, P], F32, name="bt", tag="bank5")
+        for t in range(4):
+            nc.tensor.transpose(bt[:, t, :], bias_f[:, t, :], ident[:])
+        patches(1)
+        nc.vector.tensor_copy(out=bias_t[:], in_=bt[:, :, 0:NB].rearrange("m t c -> m c t"))
+        flip(2)
+        flip(3)
+        flip(4)
+        quantise(0, 4)
+        quantise(4, 8)
+        quantise(8, 9)
+
+        acc = [psum.tile([P, NT], F32, name="acc%d" % c, tag="bank%d" % c) for c in range(NB)]
+
+        def w_operands(g, c):
+            cols = slice(NT * c, NT * (c + 1))
+            if g < G_HEAD:
+                words = w_head[g][:, cols]
+            else:
+                words = w_tail[:, g - G_HEAD, cols]
+            if g < 8:
+                plane = plane_a if g < 4 else plane_b
+                return words, plane[4 * (g % 4) : P, cols]
+            return words, plane_c[4 * (c // 2) : P, NT * (c % 2) : NT * (c % 2 + 1)]
+
+        def mx(g, c):
+            words, scales = w_operands(g, c)
+            nc.tensor.matmul_mx(
+                out=acc[c][:],
+                lhsT=a_codes[:, g, :].bitcast(FP8X4),
+                lhsT_scale=a_scales[:, g, :],
+                rhs=words.bitcast(FP8X4),
+                rhs_scale=scales,
+                start=(g == 0),
+                stop=(g == G - 1),
+            )
+
+        for g in range(G_HEAD):
+            for c in range(NB):
+                mx(g, c)
+
+        y_tiles = {}
+
+        def close(chunk):
+            for c in chunk:
+                for g in range(G_HEAD, G):
+                    mx(g, c)
+                y = ypool.tile([P, 4, P], F32, name="y")
+                nc.scalar.copy(out=y[:], in_=acc[c][:].rearrange("p (m t) -> p t m", t=4))
+                y_tiles[c] = y
+
+        def leave(chunk):
+            for c in chunk:
+                yt = psum.tile([P, 4, P], F32, name="yt%d" % c, tag="bank%d" % c)
+                for t in range(4):
+                    nc.tensor.transpose(yt[:, t, :], y_tiles[c][:, t, :], ident[:])
+                o = opool.tile([P, 2, 4, 64], F32, name="o")
+                nc.vector.tensor_tensor(
+                    out=o[:],
+                    in0=yt[:].rearrange("m t (b r) -> m b t r", b=2),
+                    in1=bias_t[:, c, :].unsqueeze(1).unsqueeze(3).to_broadcast([P, 2, 4, 64]),
+                    op=mybir.AluOpType.add,
+                )
+                nc.sync.dma_start(out=ov[c], in_=o[:].rearrange("m b t r -> m b (t r)"))
+
+        close(TAIL_CHUNKS[0])
+        for n in range(1, len(TAIL_CHUNKS)):
+            close(TAIL_CHUNKS[n])
+            leave(TAIL_CHUNKS[n - 1])
+        leave(TAIL_CHUNKS[-1])

@@ -58,8 +58,7 @@ def tile_conv2d_w_kernel(tc, x, weights_words, weights_scales, bias, out):
         make_identity(nc, ident[:])
         nc.gpsimd.memset(bias_f[:], 0.0)
 
-        for dj in range(3):
-            nc.sync.dma_start(out=xs[:, dj, 0:798], in_=xf[:, dj : dj + 798])
+        nc.sync.dma_start(out=xs[:, 0, :], in_=xf)
         nc.scalar.dma_start(out=bias_raw[0:NB, :], in_=bias.rearrange("(c n) -> c n", c=NB))
         for plane, g0 in ((plane_a, 0), (plane_b, 4)):
             for q in (0, 2, 1, 3):
@@ -116,6 +115,8 @@ def tile_conv2d_w_kernel(tc, x, weights_words, weights_scales, bias, out):
                 in_=grouped[:, g0:g1].rearrange("p g c t -> p (g c t)"),
             )
 
+        nc.scalar.copy(out=xs[:, 1, 0:798], in_=xs[:, 0, 1:799])
+        nc.vector.tensor_copy(out=xs[:, 2, 0:798], in_=xs[:, 0, 2:800])
         patches(0)
         flip(0)
         flip(1)

@@ -35,7 +35,7 @@ def tile_conv2d_w_kernel(tc, x, weights_words, weights_scales, bias, out):
         sc = weights_scales.bitcast(I32)
         ov = out.rearrange("b (c m t) u v -> c m b (t u v)", c=NB, m=P, t=4)
 
-        xs = keep.tile([P, 3, 800], BF16, name="xs")
+        xs = keep.tile([P, 3, 800], BF16, name="xs", align_bytes=256)
         a_rows = keep.tile([P, 4608], BF16, name="a_rows", align_bytes=64)
         grouped = keep.tile([P, G, P, 4], BF16, name="grouped", align_bytes=64)
         a_codes = keep.tile([P, G, P], U32, name="a_codes", align_bytes=64)
@@ -44,13 +44,13 @@ def tile_conv2d_w_kernel(tc, x, weights_words, weights_scales, bias, out):
         bias_raw = keep.tile([P, NT], BF16, name="bias_raw")
         bias_f = keep.tile([P, 4, P], F32, name="bias_f")
         bias_t = keep.tile([P, NB, 4], F32, name="bias_t")
-        plane_a = keep.tile([P, CO], U8, name="plane_a", align_bytes=64)
-        plane_b = keep.tile([P, CO], U8, name="plane_b", align_bytes=64)
-        plane_c = keep.tile([P, CO // 4], U8, name="plane_c", align_bytes=64)
+        plane_a = keep.tile([P, CO], U8, name="plane_a", align_bytes=256)
+        plane_b = keep.tile([P, CO], U8, name="plane_b", align_bytes=256)
+        plane_c = keep.tile([P, CO // 4], U8, name="plane_c", align_bytes=256)
         w_head = [
-            keep.tile([P, CO], I32, name="w_head%d" % g, align_bytes=64) for g in range(G_HEAD)
+            keep.tile([P, CO], I32, name="w_head%d" % g, align_bytes=256) for g in range(G_HEAD)
         ]
-        w_tail = keep.tile([P, G - G_HEAD, CO], I32, name="w_tail", align_bytes=64)
+        w_tail = keep.tile([P, G - G_HEAD, CO], I32, name="w_tail", align_bytes=256)
 
         nc.vector.memset(plane_a[:].bitcast(I32), 0)
         nc.vector.memset(plane_b[:].bitcast(I32), 0)
@@ -179,7 +179,7 @@ def tile_conv2d_w_kernel(tc, x, weights_words, weights_scales, bias, out):
                 yt = psum.tile([P, 4, P], F32, name="yt%d" % c, tag="bank%d" % c)
                 for t in range(4):
                     nc.tensor.transpose(yt[:, t, :], y_tiles[c][:, t, :], ident[:])
-                o = opool.tile([P, 2, 4, 64], F32, name="o")
+                o = opool.tile([P, 2, 4, 64], F32, name="o", align_bytes=256)
                 nc.vector.tensor_tensor(
                     out=o[:],
                     in0=yt[:].rearrange("m t (b r) -> m b t r", b=2),

@@ -25,15 +25,12 @@ def tile_conv2d_w_kernel(tc, x, weights_words, weights_scales, bias, out):
     nc = tc.nc
     with ExitStack() as ctx:
         keep = ctx.enter_context(tc.tile_pool(name="keep", bufs=1))
-        ypool = ctx.enter_context(tc.tile_pool(name="ypool", bufs=8))
-        opool = ctx.enter_context(tc.tile_pool(name="opool", bufs=8))
         psum = ctx.enter_context(tc.psum_pool(name="psum", bufs=1))
         ctx.enter_context(tc.manual_schedule())
 
         xf = x.rearrange("b (r c) h w -> (b r) (c h w)", c=8)
         ww = weights_words.rearrange("g p n t -> g p (n t)").bitcast(I32)
         sc = weights_scales.bitcast(I32)
-        ov = out.rearrange("b (c m t) u v -> c m b (t u v)", c=NB, m=P, t=4)
 
         xs = keep.tile([P, 3, 800], BF16, name="xs", align_bytes=256)
         a_rows = keep.tile([P, 4608], BF16, name="a_rows", align_bytes=64)
@@ -44,6 +41,9 @@ def tile_conv2d_w_kernel(tc, x, weights_words, weights_scales, bias, out):
         bias_raw = keep.tile([P, NT], BF16, name="bias_raw")
         bias_f = keep.tile([P, 4, P], F32, name="bias_f")
         bias_t = keep.tile([P, NB, 4], F32, name="bias_t")
+        bias_raw2 = keep.tile([P, 2 * NT], BF16, name="bias_raw2")
+        bias_f2 = keep.tile([P, 8, P], F32, name="bias_f2")
+        bias_t2 = keep.tile([P, NB // 2, 8], F32, name="bias_t2")
         plane_a = keep.tile([P, CO], U8, name="plane_a", align_bytes=256)
         plane_b = keep.tile([P, CO], U8, name="plane_b", align_bytes=256)
         plane_c = keep.tile([P, CO // 4], U8, name="plane_c", align_bytes=256)
@@ -57,9 +57,13 @@ def tile_conv2d_w_kernel(tc, x, weights_words, weights_scales, bias, out):
         nc.vector.memset(plane_c[:].bitcast(I32), 0)
         make_identity(nc, ident[:])
         nc.gpsimd.memset(bias_f[:], 0.0)
+        nc.gpsimd.memset(bias_f2[:], 0.0)
 
         nc.sync.dma_start(out=xs[:, 0, :], in_=xf)
         nc.scalar.dma_start(out=bias_raw[0:NB, :], in_=bias.rearrange("(c n) -> c n", c=NB))
+        nc.scalar.dma_start(
+            out=bias_raw2[0 : NB // 2, :], in_=bias.rearrange("(c n) -> c n", c=NB // 2)
+        )
         for plane, g0 in ((plane_a, 0), (plane_b, 4)):
             for q in (0, 2, 1, 3):
                 nc.sync.dma_start(
@@ -126,8 +130,20 @@ def tile_conv2d_w_kernel(tc, x, weights_words, weights_scales, bias, out):
         bt = psum.tile([P, 4, P], F32, name="bt", tag="bank5")
         for t in range(4):
             nc.tensor.transpose(bt[:, t, :], bias_f[:, t, :], ident[:])
+        nc.vector.tensor_copy(
+            out=bias_f2[0 : NB // 2], in_=bias_raw2[0 : NB // 2, :].rearrange("c (m t) -> c t m", t=8)
+        )
+        bt2 = [psum.tile([P, 4, P], F32, name="bt2%d" % h, tag="bank%d" % (6 + h)) for h in range(2)]
+        for h in range(2):
+            for t in range(4):
+                nc.tensor.transpose(bt2[h][:, t, :], bias_f2[:, 4 * h + t, :], ident[:])
         patches(1)
         nc.vector.tensor_copy(out=bias_t[:], in_=bt[:, :, 0:NB].rearrange("m t c -> m c t"))
+        for h in range(2):
+            nc.vector.tensor_copy(
+                out=bias_t2[:, :, 4 * h : 4 * h + 4],
+                in_=bt2[h][:, :, 0 : NB // 2].rearrange("m t c -> m c t"),
+            )
         flip(2)
         flip(3)
         flip(4)
@@ -167,26 +183,41 @@ def tile_conv2d_w_kernel(tc, x, weights_words, weights_scales, bias, out):
         y_tiles = {}
 
         def close(chunk):
-            for c in chunk:
+            banks = len(chunk)
+            y = keep.tile([P, 4 * banks, P], F32, name="y%d" % chunk[0])
+            for h, c in enumerate(chunk):
                 for g in range(G_HEAD, G):
                     mx(g, c)
-                y = ypool.tile([P, 4, P], F32, name="y")
-                nc.scalar.copy(out=y[:], in_=acc[c][:].rearrange("p (m t) -> p t m", t=4))
-                y_tiles[c] = y
+                nc.scalar.copy(
+                    out=y[:, :, (P // banks) * h : (P // banks) * (h + 1)],
+                    in_=acc[c][:].rearrange("p (m t) -> p t m", t=4 * banks),
+                )
+            y_tiles[chunk[0]] = y
 
         def leave(chunk):
-            for c in chunk:
+            banks = len(chunk)
+            y = y_tiles[chunk[0]]
+            o = keep.tile([P, 2, 4 * banks, 64], F32, name="o%d" % chunk[0], align_bytes=256)
+            for h, c in enumerate(chunk):
                 yt = psum.tile([P, 4, P], F32, name="yt%d" % c, tag="bank%d" % c)
                 for t in range(4):
-                    nc.tensor.transpose(yt[:, t, :], y_tiles[c][:, t, :], ident[:])
-                o = opool.tile([P, 2, 4, 64], F32, name="o", align_bytes=256)
+                    nc.tensor.transpose(yt[:, t, :], y[:, 4 * h + t, :], ident[:])
+                if banks == 1:
+                    bias_cols = bias_t[:, c, :]
+                else:
+                    bias_cols = bias_t2[:, c // 2, 4 * h : 4 * h + 4]
                 nc.vector.tensor_tensor(
-                    out=o[:],
+                    out=o[:, :, 4 * h : 4 * h + 4, :],
                     in0=yt[:].rearrange("m t (b r) -> m b t r", b=2),
-                    in1=bias_t[:, c, :].unsqueeze(1).unsqueeze(3).to_broadcast([P, 2, 4, 64]),
+                    in1=bias_cols.unsqueeze(1).unsqueeze(3).to_broadcast([P, 2, 4, 64]),
                     op=mybir.AluOpType.add,
                 )
-                nc.sync.dma_start(out=ov[c], in_=o[:].rearrange("m b t r -> m b (t r)"))
+            nc.sync.dma_start(
+                out=out[:, NT * chunk[0] : NT * (chunk[-1] + 1)].rearrange(
+                    "b (m t) u v -> m b (t u v)", t=4 * banks
+                ),
+                in_=o[:].rearrange("m b t r -> m b (t r)"),
+            )
 
         close(TAIL_CHUNKS[0])
         for n in range(1, len(TAIL_CHUNKS)):

@@ -64,17 +64,18 @@ def tile_conv2d_w_kernel(tc, x, weights_words, weights_scales, bias, out):
         nc.scalar.dma_start(
             out=bias_raw2[0 : NB // 2, :], in_=bias.rearrange("(c n) -> c n", c=NB // 2)
         )
-        for plane, g0 in ((plane_a, 0), (plane_b, 4)):
-            for q in (0, 2, 1, 3):
+        for half in ((2, 3), (0, 1)):
+            for plane, g0 in ((plane_a, 0), (plane_b, 4)):
+                for q in half:
+                    nc.sync.dma_start(
+                        out=plane[32 * q : 32 * q + 16, :].bitcast(I32),
+                        in_=sc[g0 : g0 + 4, 4 * q : 4 * q + 4, :],
+                    )
+            for q in half:
                 nc.sync.dma_start(
-                    out=plane[32 * q : 32 * q + 16, :].bitcast(I32),
-                    in_=sc[g0 : g0 + 4, 4 * q : 4 * q + 4, :],
+                    out=plane_c[32 * q : 32 * q + 16, :].bitcast(I32),
+                    in_=sc[8, 4 * q : 4 * q + 4, :].rearrange("r (c n) -> c r n", c=4),
                 )
-        for q in (0, 2, 1, 3):
-            nc.sync.dma_start(
-                out=plane_c[32 * q : 32 * q + 16, :].bitcast(I32),
-                in_=sc[8, 4 * q : 4 * q + 4, :].rearrange("r (c n) -> c r n", c=4),
-            )
         for g in range(G_HEAD):
             nc.sync.dma_start(out=w_head[g][:], in_=ww[g])
         for chunk in TAIL_CHUNKS:

from contextlib import ExitStack

import concourse.mybir as mybir
from concourse.masks import make_identity

F32 = mybir.dt.float32
BF16 = mybir.dt.bfloat16
I32 = mybir.dt.int32
U32 = mybir.dt.uint32
U8 = mybir.dt.uint8
FP8X4 = mybir.dt.float8_e4m3fn_x4

P = 128
G = 9
CO = 4096
NB = 8
NT = 512
FLOPS = 2 * 128 * 4608 * 4096

TAIL_CHUNKS = [[0, 1], [2, 3], [4, 5], [6], [7]]
G_HEAD = 7


def tile_conv2d_w_kernel(tc, x, weights_words, weights_scales, bias, out):
    nc = tc.nc
    with ExitStack() as ctx:
        keep = ctx.enter_context(tc.tile_pool(name="keep", bufs=1))
        psum = ctx.enter_context(tc.psum_pool(name="psum", bufs=1))
        ctx.enter_context(tc.manual_schedule())

        xf = x.rearrange("b (r c) h w -> (b r) (c h w)", c=8)
        ww = weights_words.rearrange("g p n t -> g p (n t)").bitcast(I32)
        sc = weights_scales.bitcast(I32)

        xs = keep.tile([P, 3, 800], BF16, name="xs", align_bytes=256)
        a_rows = keep.tile([P, 4608], BF16, name="a_rows", align_bytes=64)
        grouped = keep.tile([P, G, P, 4], BF16, name="grouped", align_bytes=64)
        a_codes = keep.tile([P, G, P], U32, name="a_codes", align_bytes=64)
        a_scales = keep.tile([P, G, P], U8, name="a_scales", align_bytes=64)
        ident = keep.tile([P, P], F32, name="ident")
        bias_raw = keep.tile([P, NT], BF16, name="bias_raw")
        bias_f = keep.tile([P, 4, P], F32, name="bias_f")
        bias_t = keep.tile([P, NB, 4], F32, name="bias_t")
        bias_raw2 = keep.tile([P, 2 * NT], BF16, name="bias_raw2")
        bias_f2 = keep.tile([P, 8, P], F32, name="bias_f2")
        bias_t2 = keep.tile([P, NB // 2, 8], F32, name="bias_t2")
        plane_a = keep.tile([P, CO], U8, name="plane_a", align_bytes=256)
        plane_b = keep.tile([P, CO], U8, name="plane_b", align_bytes=256)
        plane_c = keep.tile([P, CO // 4], U8, name="plane_c", align_bytes=256)
        w_head = [
            keep.tile([P, CO], I32, name="w_head%d" % g, align_bytes=256) for g in range(G_HEAD)
        ]
        w_tail = keep.tile([P, G - G_HEAD, CO], I32, name="w_tail", align_bytes=256)

        nc.vector.memset(plane_a[:].bitcast(I32), 0)
        nc.vector.memset(plane_b[:].bitcast(I32), 0)
        nc.vector.memset(plane_c[:].bitcast(I32), 0)
        make_identity(nc, ident[:])
        nc.gpsimd.memset(bias_f[:], 0.0)
        nc.gpsimd.memset(bias_f2[:], 0.0)

        nc.sync.dma_start(out=xs[:, 0, :], in_=xf)
        nc.scalar.dma_start(out=bias_raw[0:NB, :], in_=bias.rearrange("(c n) -> c n", c=NB))
        nc.scalar.dma_start(
            out=bias_raw2[0 : NB // 2, :], in_=bias.rearrange("(c n) -> c n", c=NB // 2)
        )
        for half in ((2, 3), (0, 1)):
            for plane, g0 in ((plane_a, 0), (plane_b, 4)):
                for q in half:
                    nc.sync.dma_start(
                        out=plane[32 * q : 32 * q + 16, :].bitcast(I32),
                        in_=sc[g0 : g0 + 4, 4 * q : 4 * q + 4, :],
                    )
            for q in half:
                nc.sync.dma_start(
                    out=plane_c[32 * q : 32 * q + 16, :].bitcast(I32),
                    in_=sc[8, 4 * q : 4 * q + 4, :].rearrange("r (c n) -> c r n", c=4),
                )
        for g in range(G_HEAD):
            nc.sync.dma_start(out=w_head[g][:], in_=ww[g])
        for chunk in TAIL_CHUNKS:
            cols = slice(NT * chunk[0], NT * (chunk[-1] + 1))
            nc.sync.dma_start(
                out=w_tail[:, :, cols], in_=ww[G_HEAD:G, :, cols].rearrange("g p n -> p g n")
            )

        xv = xs[:].rearrange("p b (c h w) -> p b c h w", c=8, h=10, w=10)
        av = a_rows[:].rearrange("p (c i j a b) -> p c i j a b", c=8, i=8, j=8, a=3, b=3)
        a_words = a_rows[:].bitcast(F32)
        g_words = grouped[:].rearrange("p g c t -> p (g c t)").bitcast(F32).rearrange(
            "p (g c u) -> p g c u", g=G, c=P, u=2
        )

        def patches(half):
            for i in range(8):
                nc.vector.tensor_copy(
                    out=av[:, 4 * half : 4 * half + 4, i],
                    in_=xv[:, :, 4 * half : 4 * half + 4, i : i + 3, 0:8].rearrange(
                        "p b c a j -> p c j a b"
                    ),
                )

        def flip(pair):
            gs = [g for g in (2 * pair, 2 * pair + 1) if g < G]
            xt = psum.tile([P, 2, 2, P], F32, name="xt%d" % pair, tag="bank%d" % pair)
            for s, g in enumerate(gs):
                for u in range(2):
                    nc.tensor.transpose(
                        xt[:, s, u, :], a_words[:, 256 * g + u : 256 * (g + 1) : 2], ident[:]
                    )
            nc.scalar.copy(
                out=g_words[:, gs[0] : gs[-1] + 1],
                in_=xt[:, 0 : len(gs)].rearrange("p g u c -> p g c u"),
            )

        def quantise(g0, g1):
            nc.vector.quantize_mx(
                out=a_codes[:, g0:g1, :].rearrange("p g c -> p (g c)").bitcast(FP8X4),
                scales=a_scales[:, g0:g1, :].rearrange("p g c -> p (g c)"),
                in_=grouped[:, g0:g1].rearrange("p g c t -> p (g c t)"),
            )

        nc.scalar.copy(out=xs[:, 1, 0:798], in_=xs[:, 0, 1:799])
        nc.vector.tensor_copy(out=xs[:, 2, 0:798], in_=xs[:, 0, 2:800])
        patches(0)
        flip(0)
        flip(1)
        nc.vector.tensor_copy(
            out=bias_f[0:NB], in_=bias_raw[0:NB, :].rearrange("c (m t) -> c t m", t=4)
        )
        bt = psum.tile([P, 4, P], F32, name="bt", tag="bank5")
        for t in range(4):
            nc.tensor.transpose(bt[:, t, :], bias_f[:, t, :], ident[:])
        nc.vector.tensor_copy(
            out=bias_f2[0 : NB // 2], in_=bias_raw2[0 : NB // 2, :].rearrange("c (m t) -> c t m", t=8)
        )
        bt2 = [psum.tile([P, 4, P], F32, name="bt2%d" % h, tag="bank%d" % (6 + h)) for h in range(2)]
        for h in range(2):
            for t in range(4):
                nc.tensor.transpose(bt2[h][:, t, :], bias_f2[:, 4 * h + t, :], ident[:])
        patches(1)
        nc.vector.tensor_copy(out=bias_t[:], in_=bt[:, :, 0:NB].rearrange("m t c -> m c t"))
        for h in range(2):
            nc.vector.tensor_copy(
                out=bias_t2[:, :, 4 * h : 4 * h + 4],
                in_=bt2[h][:, :, 0 : NB // 2].rearrange("m t c -> m c t"),
            )
        flip(2)
        flip(3)
        flip(4)
        quantise(0, 4)
        quantise(4, 8)
        quantise(8, 9)

        acc = [psum.tile([P, NT], F32, name="acc%d" % c, tag="bank%d" % c) for c in range(NB)]

        def w_operands(g, c):
            cols = slice(NT * c, NT * (c + 1))
            if g < G_HEAD:
                words = w_head[g][:, cols]
            else:
                words = w_tail[:, g - G_HEAD, cols]
            if g < 8:
                plane = plane_a if g < 4 else plane_b
                return words, plane[4 * (g % 4) : P, cols]
            return words, plane_c[4 * (c // 2) : P, NT * (c % 2) : NT * (c % 2 + 1)]

        def mx(g, c):
            words, scales = w_operands(g, c)
            nc.tensor.matmul_mx(
                out=acc[c][:],
                lhsT=a_codes[:, g, :].bitcast(FP8X4),
                lhsT_scale=a_scales[:, g, :],
                rhs=words.bitcast(FP8X4),
                rhs_scale=scales,
                start=(g == 0),
                stop=(g == G - 1),
            )

        for g in range(G_HEAD):
            for c in range(NB):
                mx(g, c)

        y_tiles = {}

        def close(chunk):
            banks = len(chunk)
            y = keep.tile([P, 4 * banks, P], F32, name="y%d" % chunk[0])
            for h, c in enumerate(chunk):
                for g in range(G_HEAD, G):
                    mx(g, c)
                nc.scalar.copy(
                    out=y[:, :, (P // banks) * h : (P // banks) * (h + 1)],
                    in_=acc[c][:].rearrange("p (m t) -> p t m", t=4 * banks),
                )
            y_tiles[chunk[0]] = y

        def leave(chunk):
            banks = len(chunk)
            y = y_tiles[chunk[0]]
            o = keep.tile([P, 2, 4 * banks, 64], F32, name="o%d" % chunk[0], align_bytes=256)
            for h, c in enumerate(chunk):
                yt = psum.tile([P, 4, P], F32, name="yt%d" % c, tag="bank%d" % c)
                for t in range(4):
                    nc.tensor.transpose(yt[:, t, :], y[:, 4 * h + t, :], ident[:])
                if banks == 1:
                    bias_cols = bias_t[:, c, :]
                else:
                    bias_cols = bias_t2[:, c // 2, 4 * h : 4 * h + 4]
                nc.vector.tensor_tensor(
                    out=o[:, :, 4 * h : 4 * h + 4, :],
                    in0=yt[:].rearrange("m t (b r) -> m b t r", b=2),
                    in1=bias_cols.unsqueeze(1).unsqueeze(3).to_broadcast([P, 2, 4, 64]),
                    op=mybir.AluOpType.add,
                )
            nc.sync.dma_start(
                out=out[:, NT * chunk[0] : NT * (chunk[-1] + 1)].rearrange(
                    "b (m t) u v -> m b (t u v)", t=4 * banks
                ),
                in_=o[:].rearrange("m b t r -> m b (t r)"),
            )

        close(TAIL_CHUNKS[0])
        for n in range(1, len(TAIL_CHUNKS)):
            close(TAIL_CHUNKS[n])
            leave(TAIL_CHUNKS[n - 1])
        leave(TAIL_CHUNKS[-1])
